import numpy as np
import ml_dtypes


BF16 = ml_dtypes.bfloat16


def bf(x):
    return np.asarray(x, np.float32).astype(BF16)


def f64(x):
    return np.asarray(x).astype(np.float64)


E2M1 = np.array([0.0, 0.5, 1.0, 1.5, 2.0, 3.0, 4.0, 6.0, -0.0, -0.5, -1.0, -1.5, -2.0, -3.0, -4.0, -6.0])


def pack_weight(w, fmt):
    k, n = w.shape
    w = f64(bf(w)).reshape(k // 32, 32, n)
    amax = np.abs(w).max(1)
    if fmt == "e4m3":
        byte = np.frexp(amax)[1] - 1 + 127 - 7
    else:
        mant, ex = np.frexp(amax / 6.0)
        byte = np.where(mant > 0.5, ex, ex - 1) + 127
    byte = np.clip(np.where(amax > 0, byte, 1), 1, 254)
    scaled = (w * np.exp2(127.0 - byte)[:, None, :]).reshape(k, n).astype(np.float32)
    by_word = np.ascontiguousarray(scaled.reshape(k // 512, 128, 4, n).transpose(0, 1, 3, 2))
    if fmt == "e4m3":
        words = by_word.astype(ml_dtypes.float8_e4m3fn).view(np.uint8)
    else:
        c = by_word.astype(ml_dtypes.float4_e2m1fn).view(np.uint8) & 0xF
        words = c[..., 0::2] | (c[..., 1::2] << 4)
    return np.ascontiguousarray(words), np.ascontiguousarray(byte.astype(np.uint8).reshape(k // 512, 16, n))


def unpack_weight(words, scales, fmt):
    g, p, n, _ = words.shape
    if fmt == "e4m3":
        vals = np.ascontiguousarray(words).view(ml_dtypes.float8_e4m3fn).astype(np.float64)
    else:
        nib = np.empty((g, p, n, 4), np.uint8)
        nib[..., 0::2] = words & 0xF
        nib[..., 1::2] = words >> 4
        vals = E2M1[nib]
    vals = vals * np.repeat(np.exp2(scales.astype(np.float64) - 127.0), 8, axis=1)[..., None]
    return vals.transpose(0, 1, 3, 2).reshape(g * 512, n)

def pack4(w):
    words, scales = pack_weight(w, "e2m1")
    return words.reshape(words.shape[0], 128, -1), scales


def unpack4(words, scales):
    return unpack_weight(words.reshape(words.shape[0], 128, -1, 2), scales, "e2m1")


def kspread(k):
    return np.exp2(np.repeat(np.random.randint(-6, 7, k // 32), 32).astype(np.float64))


B, S, D_MODEL, N_HEADS, QK_ROPE, QK_NOPE, KV_LORA, V_DIM = 2, 512, 4096, 16, 128, 128, 512, 128
QK_DIM = QK_ROPE + QK_NOPE
ROPE_BASE = 10000.0


def apply_rope(r):
    freqs = 1.0 / (ROPE_BASE ** (np.arange(0, QK_ROPE, 2) / QK_ROPE))
    t = np.arange(S)[:, None] * freqs[None, :]
    cos = np.cos(t)[None, :, None, :]
    sin = np.sin(t)[None, :, None, :]
    r1 = r[..., 0::2]
    r2 = r[..., 1::2]
    return np.stack([r1 * cos - r2 * sin, r2 * cos + r1 * sin], axis=-1).reshape(r.shape)


def setup_inputs():
    s = kspread(D_MODEL)
    x = np.random.standard_normal((B, S, D_MODEL)) * s
    x_words, x_scales = pack4(np.ascontiguousarray(x.reshape(B * S, D_MODEL).T))
    words, scales = pack4(np.random.standard_normal((D_MODEL, N_HEADS * QK_DIM)) / np.sqrt(D_MODEL) / s[:, None])
    return {"x_words": x_words, "x_scales": x_scales, "Wq_words": words, "Wq_scales": scales}


def reference(x_words, x_scales, Wq_words, Wq_scales):
    q = (unpack4(x_words, x_scales).T.reshape(B, S, D_MODEL) @ unpack4(Wq_words, Wq_scales)).reshape(B, S, N_HEADS, QK_DIM)
    q_nope, q_rope = q[..., :QK_NOPE], q[..., QK_NOPE:]
    return np.concatenate([q_nope, apply_rope(q_rope)], axis=-1)

@@ -1,0 +1,208 @@
+from contextlib import ExitStack
+
+import concourse.mybir as mybir
+
+FLOPS = 2 * 1024 * 4096 * 4096
+
+F32 = mybir.dt.float32
+BF16 = mybir.dt.bfloat16
+I32 = mybir.dt.int32
+U8 = mybir.dt.uint8
+FP4X4 = mybir.dt.float4_e2m1fn_x4
+ALU = mybir.AluOpType
+ACT = mybir.ActivationFunctionType
+
+PI = 3.141592653589793
+ROPE_BASE = 10000.0
+
+P = 128
+PASSES = 8
+TOKEN_BLOCKS = 8
+COL_BLOCKS = 8
+N = 512
+RUNS = ((0, 2), (2, 5), (5, 8))
+
+
+def tile_multiheadlatentattention_pb_kernel(tc, x_words, x_scales, Wq_words, Wq_scales, out):
+    nc = tc.nc
+    out2d = out.rearrange("b s h d -> (b s) (h d)")
+
+    with ExitStack() as ctx:
+        ctx.enter_context(tc.manual_schedule())
+        keep = ctx.enter_context(tc.tile_pool(name="keep", bufs=1))
+        opool = ctx.enter_context(tc.tile_pool(name="opool", bufs=8))
+        tpool = ctx.enter_context(tc.tile_pool(name="tpool", bufs=4))
+        psum = ctx.enter_context(tc.psum_pool(name="psum", bufs=8))
+
+        def load_planes(dst, src, g0, g1, c0, c1):
+            for q in range(4):
+                nc.sync.dma_start(
+                    out=dst[32 * q : 32 * q + 4, :, :].bitcast(I32),
+                    in_=src[g0:g1, 4 * q : 4 * q + 4, c0:c1].rearrange("g r n -> r g n").bitcast(I32),
+                )
+
+        xc = []
+        wc0 = []
+        for g in range(PASSES):
+            xc.append(keep.tile([P, 2 * 1024], U8, name="xc%d" % g, align_bytes=64))
+            wc0.append(keep.tile([P, 2 * N], U8, name="wc0_%d" % g, align_bytes=64))
+        xs = []
+        ws0 = []
+        for r in range(len(RUNS)):
+            ng = RUNS[r][1] - RUNS[r][0]
+            xs.append(keep.tile([P, ng, 1024], U8, name="xs%d" % r, align_bytes=64))
+            ws0.append(keep.tile([P, ng, N], U8, name="ws0_%d" % r, align_bytes=64))
+        wc = [None]
+        ws = [None]
+        for cb in range(1, COL_BLOCKS):
+            wc.append(keep.tile([P, PASSES, 2 * N], U8, name="wc%d" % cb, align_bytes=64))
+            ws.append(keep.tile([P, PASSES, N], U8, name="ws%d" % cb, align_bytes=64))
+
+        def run_of(g):
+            for r in range(len(RUNS)):
+                if RUNS[r][0] <= g < RUNS[r][1]:
+                    return r, g - RUNS[r][0]
+            raise ValueError("pass out of range")
+
+        def load_codes0(g):
+            nc.sync.dma_start(out=xc[g][:].bitcast(I32), in_=x_words[g].bitcast(I32))
+            nc.sync.dma_start(out=wc0[g][:].bitcast(I32), in_=Wq_words[g, :, 0 : 2 * N].bitcast(I32))
+
+        def load_planes0(r):
+            g0, g1 = RUNS[r]
+            load_planes(xs[r], x_scales, g0, g1, 0, 1024)
+            load_planes(ws0[r], Wq_scales, g0, g1, 0, N)
+
+        def load_col_block(cb):
+            load_planes(ws[cb], Wq_scales, 0, PASSES, cb * N, (cb + 1) * N)
+            nc.sync.dma_start(
+                out=wc[cb][:].bitcast(I32),
+                in_=Wq_words[:, :, cb * 2 * N : (cb + 1) * 2 * N].rearrange("g p n -> p g n").bitcast(I32),
+            )
+
+        for r in range(len(RUNS)):
+            nc.vector.memset(xs[r][:].bitcast(I32), 0)
+            nc.vector.memset(ws0[r][:].bitcast(I32), 0)
+        for cb in range(1, COL_BLOCKS):
+            nc.vector.memset(ws[cb][:].bitcast(I32), 0)
+
+        load_codes0(0)
+        load_planes0(0)
+        load_codes0(1)
+        load_planes0(1)
+        load_codes0(2)
+        load_codes0(3)
+        load_codes0(4)
+        load_planes0(2)
+        load_codes0(5)
+        load_codes0(6)
+        load_codes0(7)
+        load_col_block(1)
+        load_col_block(2)
+
+        pos_i = keep.tile([P, 4], I32, name="pos_i")
+        nc.gpsimd.iota(pos_i[:], pattern=[[128, 4]], base=0, channel_multiplier=1)
+        pos_f = keep.tile([P, 4], F32, name="pos_f")
+        nc.vector.tensor_copy(out=pos_f[:], in_=pos_i[:])
+        turns = keep.tile([P, 4], F32, name="turns")
+        nc.vector.tensor_scalar_mul(out=turns[:], in0=pos_f[:], scalar1=1.0 / (2.0 * PI))
+        freq = keep.tile([P, 64], F32, name="freq")
+        nc.vector.memset(freq[:, 0:1], 1.0)
+        for k in range(6):
+            n = 2**k
+            nc.vector.tensor_scalar_mul(out=freq[:, n : 2 * n], in0=freq[:, 0:n], scalar1=ROPE_BASE ** (-n / 64.0))
+        gdup = keep.tile([P, 2, 64, 2], F32, name="gdup")
+        phase = keep.tile([P, 2, 64, 2], F32, name="phase")
+        for w in range(2):
+            for e in range(2):
+                nc.vector.tensor_copy(out=gdup[:, w, :, e], in_=freq[:])
+        nc.vector.memset(phase[:, 0, :, :], 0.0)
+        nc.vector.memset(phase[:, 1, :, 0], -0.25)
+        nc.vector.memset(phase[:, 1, :, 1], 0.25)
+        u = keep.tile([P, 4, 256], F32, name="u")
+        for a in range(4):
+            nc.vector.scalar_tensor_tensor(
+                out=u[:, a, :],
+                in0=gdup[:].rearrange("p w i e -> p (w i e)"),
+                scalar=turns[:, a : a + 1],
+                in1=phase[:].rearrange("p w i e -> p (w i e)"),
+                op0=ALU.mult,
+                op1=ALU.add,
+            )
+        uflat = u[:].rearrange("p a j -> p (a j)")
+        k_i = keep.tile([P, 1024], I32, name="k_i")
+        nc.vector.tensor_copy(out=k_i[:], in_=uflat)
+        k_f = keep.tile([P, 1024], F32, name="k_f")
+        nc.vector.tensor_copy(out=k_f[:], in_=k_i[:])
+        red = keep.tile([P, 1024], F32, name="red")
+        nc.vector.tensor_sub(out=red[:], in0=uflat, in1=k_f[:])
+        half_sin = keep.tile([P, 1024], F32, name="half_sin")
+        nc.scalar.activation(out=half_sin[:], in_=red[:], func=ACT.Sin, scale=PI)
+        m2sq = keep.tile([P, 1024], F32, name="m2sq")
+        nc.vector.scalar_tensor_tensor(
+            out=m2sq[:], in0=half_sin[:], scalar=-2.0, in1=half_sin[:], op0=ALU.mult, op1=ALU.mult
+        )
+        tab = keep.tile([P, 4, 2, 2, 128], F32, name="tab")
+        for h in range(2):
+            nc.vector.tensor_scalar_add(
+                out=tab[:].rearrange("p a w h j -> p (a w) h j")[:, :, h, :],
+                in0=m2sq[:].rearrange("p (m j) -> p m j", j=128),
+                scalar1=1.0,
+            )
+
+        def one_pass(acc, g, tb, cb):
+            r, gl = run_of(g)
+            if cb == 0:
+                rhs = wc0[g][:]
+                rhs_scale = ws0[r][:, gl, :]
+            else:
+                rhs = wc[cb][:, g, :]
+                rhs_scale = ws[cb][:, g, :]
+            nc.tensor.matmul_mx(
+                out=acc[:],
+                lhsT=xc[g][:, tb * 256 : (tb + 1) * 256].bitcast(FP4X4),
+                lhsT_scale=xs[r][:, gl, tb * 128 : (tb + 1) * 128],
+                rhs=rhs.bitcast(FP4X4),
+                rhs_scale=rhs_scale,
+                start=(g == 0),
+                stop=(g == PASSES - 1),
+            )
+
+        def epilogue(acc, tb, cb):
+            a = tb % 4
+            o = opool.tile([P, N], F32, name="o", tag="o")
+            t = tpool.tile([P, 2, 256], F32, name="t", tag="t")
+            acc4 = acc[:].rearrange("p (h c j) -> p h c j", h=2, c=2)
+            o4 = o[:].rearrange("p (h c j) -> p h c j", h=2, c=2)
+            nc.scalar.copy(out=o4[:, :, 0, :], in_=acc4[:, :, 0, :])
+            for w in range(2):
+                nc.vector.tensor_mul(
+                    out=t[:, w, :].rearrange("p (h j) -> p h j", h=2),
+                    in0=acc4[:, :, 1, :],
+                    in1=tab[:, a, w, :, :],
+                )
+            nc.vector.tensor_add(
+                out=o4[:, :, 1, :].rearrange("p h (i e) -> p h i e", e=2),
+                in0=t[:, 0, :].rearrange("p (h i e) -> p h i e", h=2, e=2),
+                in1=t[:, 1, :].rearrange("p (h i e) -> p h i e", h=2, e=2)[:, :, :, ::-1],
+            )
+            nc.sync.dma_start(out=out2d[tb * P : (tb + 1) * P, cb * N : (cb + 1) * N], in_=o[:])
+
+        first = []
+        for tb in range(TOKEN_BLOCKS):
+            first.append(psum.tile([P, N], F32, name="acc", tag="acc"))
+        for g in range(PASSES):
+            for tb in range(TOKEN_BLOCKS):
+                one_pass(first[tb], g, tb, 0)
+        for tb in range(TOKEN_BLOCKS):
+            epilogue(first[tb], tb, 0)
+        load_col_block(3)
+
+        for cb in range(1, COL_BLOCKS):
+            for tb in range(TOKEN_BLOCKS):
+                acc = psum.tile([P, N], F32, name="acc", tag="acc")
+                for g in range(PASSES):
+                    one_pass(acc, g, tb, cb)
+                epilogue(acc, tb, cb)
+            if cb + 3 < COL_BLOCKS:
+                load_col_block(cb + 3)

@@ -20,6 +20,7 @@ PASSES = 8
 TOKEN_BLOCKS = 8
 COL_BLOCKS = 8
 N = 512
+WARM = 6
 RUNS = ((0, 2), (2, 5), (5, 8))
 
 
@@ -44,7 +45,12 @@ def tile_multiheadlatentattention_pb_kernel(tc, x_words, x_scales, Wq_words, Wq_
         xc = []
         wc0 = []
         for g in range(PASSES):
-            xc.append(keep.tile([P, 2 * 1024], U8, name="xc%d" % g, align_bytes=64))
+            xc.append(
+                [
+                    keep.tile([P, 1024], U8, name="xc%d_0" % g, align_bytes=64),
+                    keep.tile([P, 1024], U8, name="xc%d_1" % g, align_bytes=64),
+                ]
+            )
             wc0.append(keep.tile([P, 2 * N], U8, name="wc0_%d" % g, align_bytes=64))
         xs = []
         ws0 = []
@@ -64,9 +70,16 @@ def tile_multiheadlatentattention_pb_kernel(tc, x_words, x_scales, Wq_words, Wq_
                     return r, g - RUNS[r][0]
             raise ValueError("pass out of range")
 
-        def load_codes0(g):
-            nc.sync.dma_start(out=xc[g][:].bitcast(I32), in_=x_words[g].bitcast(I32))
+        def load_x_half(g, b):
+            nc.sync.dma_start(out=xc[g][b][:].bitcast(I32), in_=x_words[g, :, b * 1024 : (b + 1) * 1024].bitcast(I32))
+
+        def load_w0(g):
             nc.sync.dma_start(out=wc0[g][:].bitcast(I32), in_=Wq_words[g, :, 0 : 2 * N].bitcast(I32))
+
+        def load_codes0(g):
+            load_x_half(g, 0)
+            load_w0(g)
+            load_x_half(g, 1)
 
         def load_planes0(r):
             g0, g1 = RUNS[r]
@@ -80,14 +93,19 @@ def tile_multiheadlatentattention_pb_kernel(tc, x_words, x_scales, Wq_words, Wq_
                 in_=Wq_words[:, :, cb * 2 * N : (cb + 1) * 2 * N].rearrange("g p n -> p g n").bitcast(I32),
             )
 
+        warm = keep.tile([P, N // 2], F32, name="warm")
         for r in range(len(RUNS)):
             nc.vector.memset(xs[r][:].bitcast(I32), 0)
             nc.vector.memset(ws0[r][:].bitcast(I32), 0)
+            if r == 0:
+                nc.vector.memset(warm[:], 0.0)
         for cb in range(1, COL_BLOCKS):
             nc.vector.memset(ws[cb][:].bitcast(I32), 0)
 
-        load_codes0(0)
+        load_x_half(0, 0)
+        load_w0(0)
         load_planes0(0)
+        load_x_half(0, 1)
         load_codes0(1)
         load_planes0(1)
         load_codes0(2)
@@ -99,6 +117,12 @@ def tile_multiheadlatentattention_pb_kernel(tc, x_words, x_scales, Wq_words, Wq_
         load_codes0(7)
         load_col_block(1)
         load_col_block(2)
+
+        wacc = psum.tile([P, N], F32, name="acc", tag="acc")
+        for i in range(WARM):
+            nc.tensor.matmul(
+                out=wacc[:], lhsT=warm[:].bitcast(BF16)[:, 0:P], rhs=warm[:].bitcast(BF16), start=True, stop=True
+            )
 
         pos_i = keep.tile([P, 4], I32, name="pos_i")
         nc.gpsimd.iota(pos_i[:], pattern=[[128, 4]], base=0, channel_multiplier=1)
@@ -150,17 +174,18 @@ def tile_multiheadlatentattention_pb_kernel(tc, x_words, x_scales, Wq_words, Wq_
                 scalar1=1.0,
             )
 
-        def one_pass(acc, g, tb, cb):
+        def one_pass(acc, g, tb, cb, c0, c1):
             r, gl = run_of(g)
             if cb == 0:
-                rhs = wc0[g][:]
-                rhs_scale = ws0[r][:, gl, :]
+                rhs = wc0[g][:, 2 * c0 : 2 * c1]
+                rhs_scale = ws0[r][:, gl, c0:c1]
             else:
-                rhs = wc[cb][:, g, :]
-                rhs_scale = ws[cb][:, g, :]
+                rhs = wc[cb][:, g, 2 * c0 : 2 * c1]
+                rhs_scale = ws[cb][:, g, c0:c1]
+            tl = tb % 4
             nc.tensor.matmul_mx(
-                out=acc[:],
-                lhsT=xc[g][:, tb * 256 : (tb + 1) * 256].bitcast(FP4X4),
+                out=acc,
+                lhsT=xc[g][tb // 4][:, tl * 256 : (tl + 1) * 256].bitcast(FP4X4),
                 lhsT_scale=xs[r][:, gl, tb * 128 : (tb + 1) * 128],
                 rhs=rhs.bitcast(FP4X4),
                 rhs_scale=rhs_scale,
@@ -168,41 +193,73 @@ def tile_multiheadlatentattention_pb_kernel(tc, x_words, x_scales, Wq_words, Wq_
                 stop=(g == PASSES - 1),
             )
 
-        def epilogue(acc, tb, cb):
-            a = tb % 4
-            o = opool.tile([P, N], F32, name="o", tag="o")
+        def rotate(dst, src, tb, heads):
             t = tpool.tile([P, 2, 256], F32, name="t", tag="t")
-            acc4 = acc[:].rearrange("p (h c j) -> p h c j", h=2, c=2)
-            o4 = o[:].rearrange("p (h c j) -> p h c j", h=2, c=2)
-            nc.scalar.copy(out=o4[:, :, 0, :], in_=acc4[:, :, 0, :])
             for w in range(2):
                 nc.vector.tensor_mul(
-                    out=t[:, w, :].rearrange("p (h j) -> p h j", h=2),
-                    in0=acc4[:, :, 1, :],
-                    in1=tab[:, a, w, :, :],
+                    out=t[:, w, 0 : heads * 128].rearrange("p (h j) -> p h j", h=heads),
+                    in0=src,
+                    in1=tab[:, tb % 4, w, 0:heads, :],
                 )
             nc.vector.tensor_add(
-                out=o4[:, :, 1, :].rearrange("p h (i e) -> p h i e", e=2),
-                in0=t[:, 0, :].rearrange("p (h i e) -> p h i e", h=2, e=2),
-                in1=t[:, 1, :].rearrange("p (h i e) -> p h i e", h=2, e=2)[:, :, :, ::-1],
+                out=dst.rearrange("p h (i e) -> p h i e", e=2),
+                in0=t[:, 0, 0 : heads * 128].rearrange("p (h i e) -> p h i e", h=heads, e=2),
+                in1=t[:, 1, 0 : heads * 128].rearrange("p (h i e) -> p h i e", h=heads, e=2)[:, :, :, ::-1],
             )
-            nc.sync.dma_start(out=out2d[tb * P : (tb + 1) * P, cb * N : (cb + 1) * N], in_=o[:])
+
+        def epilogue(acc, tb, cb, c0, heads):
+            width = 256 * heads
+            o = opool.tile([P, N], F32, name="o", tag="o")
+            acc4 = acc[:, 0:width].rearrange("p (h c j) -> p h c j", h=heads, c=2)
+            o4 = o[:, 0:width].rearrange("p (h c j) -> p h c j", h=heads, c=2)
+            nc.scalar.copy(out=o4[:, :, 0, :], in_=acc4[:, :, 0, :])
+            rotate(o4[:, :, 1, :], acc4[:, :, 1, :], tb, heads)
+            nc.sync.dma_start(
+                out=out2d[tb * P : (tb + 1) * P, cb * N + c0 : cb * N + c0 + width], in_=o[:, 0:width]
+            )
 
         first = []
         for tb in range(TOKEN_BLOCKS):
             first.append(psum.tile([P, N], F32, name="acc", tag="acc"))
         for g in range(PASSES):
             for tb in range(TOKEN_BLOCKS):
-                one_pass(first[tb], g, tb, 0)
+                one_pass(first[tb][:], g, tb, 0, 0, N)
         for tb in range(TOKEN_BLOCKS):
-            epilogue(first[tb], tb, 0)
+            epilogue(first[tb], tb, 0, 0, 2)
         load_col_block(3)
 
+        last_tb = TOKEN_BLOCKS - 1
+        last_cb = COL_BLOCKS - 1
         for cb in range(1, COL_BLOCKS):
             for tb in range(TOKEN_BLOCKS):
+                if cb == last_cb and tb == last_tb:
+                    break
                 acc = psum.tile([P, N], F32, name="acc", tag="acc")
                 for g in range(PASSES):
-                    one_pass(acc, g, tb, cb)
-                epilogue(acc, tb, cb)
+                    one_pass(acc[:], g, tb, cb, 0, N)
+                epilogue(acc, tb, cb, 0, 2)
             if cb + 3 < COL_BLOCKS:
                 load_col_block(cb + 3)
+
+        rows = slice(last_tb * P, (last_tb + 1) * P)
+        pieces = []
+        for c0 in (128, 384, 0, 256):
+            acc = psum.tile([P, N], F32, name="acc", tag="acc")
+            for g in range(PASSES):
+                one_pass(acc[:, 0:128], g, last_tb, last_cb, c0, c0 + 128)
+            pieces.append(acc)
+        for i in range(4):
+            c0 = (128, 384, 0, 256)[i]
+            o = opool.tile([P, N], F32, name="o", tag="o")
+            dst = out2d[rows, last_cb * N + c0 : last_cb * N + c0 + 128]
+            if i < 2:
+                rotate(
+                    o[:, 0:128].rearrange("p (h j) -> p h j", h=1),
+                    pieces[i][:, 0:128].rearrange("p (h j) -> p h j", h=1),
+                    last_tb,
+                    1,
+                )
+                nc.sync.dma_start(out=dst, in_=o[:, 0:128])
+            else:
+                nc.scalar.copy(out=o[:, 0:128], in_=pieces[i][:, 0:128])
+                nc.scalar.dma_start(out=dst, in_=o[:, 0:128])

@@ -64,6 +64,9 @@ def tile_multiheadlatentattention_pb_kernel(tc, x_words, x_scales, Wq_words, Wq_
             wc.append(keep.tile([P, PASSES, 2 * N], U8, name="wc%d" % cb, align_bytes=64))
             ws.append(keep.tile([P, PASSES, N], U8, name="ws%d" % cb, align_bytes=64))
 
+        wc_stage = keep.tile([P, PASSES, 2 * N], U8, name="wc_stage", align_bytes=64)
+        ws_stage = keep.tile([P, PASSES, N], U8, name="ws_stage", align_bytes=64)
+
         def run_of(g):
             for r in range(len(RUNS)):
                 if RUNS[r][0] <= g < RUNS[r][1]:
@@ -87,9 +90,12 @@ def tile_multiheadlatentattention_pb_kernel(tc, x_words, x_scales, Wq_words, Wq_
             load_planes(ws0[r], Wq_scales, g0, g1, 0, N)
 
         def load_col_block(cb):
-            load_planes(ws[cb], Wq_scales, 0, PASSES, cb * N, (cb + 1) * N)
+            codes, planes = wc[cb], ws[cb]
+            if cb == COL_BLOCKS - 1:
+                codes, planes = wc_stage, ws_stage
+            load_planes(planes, Wq_scales, 0, PASSES, cb * N, (cb + 1) * N)
             nc.sync.dma_start(
-                out=wc[cb][:].bitcast(I32),
+                out=codes[:].bitcast(I32),
                 in_=Wq_words[:, :, cb * 2 * N : (cb + 1) * 2 * N].rearrange("g p n -> p g n").bitcast(I32),
             )
 
@@ -99,8 +105,9 @@ def tile_multiheadlatentattention_pb_kernel(tc, x_words, x_scales, Wq_words, Wq_
             nc.vector.memset(ws0[r][:].bitcast(I32), 0)
             if r == 0:
                 nc.vector.memset(warm[:], 0.0)
-        for cb in range(1, COL_BLOCKS):
+        for cb in range(1, COL_BLOCKS - 1):
             nc.vector.memset(ws[cb][:].bitcast(I32), 0)
+        nc.vector.memset(ws_stage[:].bitcast(I32), 0)
 
         load_x_half(0, 0)
         load_w0(0)
@@ -207,16 +214,35 @@ def tile_multiheadlatentattention_pb_kernel(tc, x_words, x_scales, Wq_words, Wq_
                 in1=t[:, 1, 0 : heads * 128].rearrange("p (h i e) -> p h i e", h=heads, e=2)[:, :, :, ::-1],
             )
 
-        def epilogue(acc, tb, cb, c0, heads):
-            width = 256 * heads
+        last_cb = COL_BLOCKS - 1
+        SPLIT = 2
+
+        def regroup_last_block():
+            for c in range(2):
+                nc.vector.tensor_copy(
+                    out=wc[last_cb][:].bitcast(I32).rearrange("p s (c h w) -> p s c h w", c=2, h=2)[:, :, 1 - c, :, :],
+                    in_=wc_stage[:].bitcast(I32).rearrange("p s (h c w) -> p s h c w", h=2, c=2)[:, :, :, c, :],
+                )
+                nc.vector.tensor_copy(
+                    out=ws[last_cb][:].bitcast(I32).rearrange("p s (c h w) -> p s c h w", c=2, h=2)[:, :, 1 - c, :, :],
+                    in_=ws_stage[:].bitcast(I32).rearrange("p s (h c w) -> p s h c w", h=2, c=2)[:, :, :, c, :],
+                )
+
+        def out_block(tb, cb):
+            return out2d[tb * P : (tb + 1) * P, cb * N : (cb + 1) * N]
+
+        def epilogue(acc, tb, cb):
             o = opool.tile([P, N], F32, name="o", tag="o")
-            acc4 = acc[:, 0:width].rearrange("p (h c j) -> p h c j", h=heads, c=2)
-            o4 = o[:, 0:width].rearrange("p (h c j) -> p h c j", h=heads, c=2)
-            nc.scalar.copy(out=o4[:, :, 0, :], in_=acc4[:, :, 0, :])
-            rotate(o4[:, :, 1, :], acc4[:, :, 1, :], tb, heads)
-            nc.sync.dma_start(
-                out=out2d[tb * P : (tb + 1) * P, cb * N + c0 : cb * N + c0 + width], in_=o[:, 0:width]
-            )
+            o4 = o[:].rearrange("p (h c j) -> p h c j", h=2, c=2)
+            if cb == last_cb:
+                plain = acc[:, 256:512].rearrange("p (h j) -> p h j", h=2)
+                turned = acc[:, 0:256].rearrange("p (h j) -> p h j", h=2)
+            else:
+                plain = acc[:].rearrange("p (h c j) -> p h c j", h=2, c=2)[:, :, 0, :]
+                turned = acc[:].rearrange("p (h c j) -> p h c j", h=2, c=2)[:, :, 1, :]
+            nc.scalar.copy(out=o4[:, :, 0, :], in_=plain)
+            rotate(o4[:, :, 1, :], turned, tb, 2)
+            nc.sync.dma_start(out=out_block(tb, cb), in_=o[:])
 
         first = []
         for tb in range(TOKEN_BLOCKS):
@@ -225,41 +251,40 @@ def tile_multiheadlatentattention_pb_kernel(tc, x_words, x_scales, Wq_words, Wq_
             for tb in range(TOKEN_BLOCKS):
                 one_pass(first[tb][:], g, tb, 0, 0, N)
         for tb in range(TOKEN_BLOCKS):
-            epilogue(first[tb], tb, 0, 0, 2)
+            epilogue(first[tb], tb, 0)
         load_col_block(3)
 
-        last_tb = TOKEN_BLOCKS - 1
-        last_cb = COL_BLOCKS - 1
         for cb in range(1, COL_BLOCKS):
-            for tb in range(TOKEN_BLOCKS):
-                if cb == last_cb and tb == last_tb:
-                    break
+            whole = TOKEN_BLOCKS
+            if cb == last_cb:
+                whole = TOKEN_BLOCKS - SPLIT
+            for tb in range(whole):
                 acc = psum.tile([P, N], F32, name="acc", tag="acc")
                 for g in range(PASSES):
                     one_pass(acc[:], g, tb, cb, 0, N)
-                epilogue(acc, tb, cb, 0, 2)
+                epilogue(acc, tb, cb)
             if cb + 3 < COL_BLOCKS:
                 load_col_block(cb + 3)
+            if cb + 2 == last_cb:
+                regroup_last_block()
 
-        rows = slice(last_tb * P, (last_tb + 1) * P)
-        pieces = []
-        for c0 in (128, 384, 0, 256):
-            acc = psum.tile([P, N], F32, name="acc", tag="acc")
-            for g in range(PASSES):
-                one_pass(acc[:, 0:128], g, last_tb, last_cb, c0, c0 + 128)
-            pieces.append(acc)
-        for i in range(4):
-            c0 = (128, 384, 0, 256)[i]
+        late = range(TOKEN_BLOCKS - SPLIT, TOKEN_BLOCKS)
+        halves = {}
+        for c0 in (0, 256):
+            for tb in late:
+                acc = psum.tile([P, N], F32, name="acc", tag="acc")
+                for g in range(PASSES):
+                    one_pass(acc[:, 0:256], g, tb, last_cb, c0, c0 + 256)
+                halves[(c0, tb)] = acc
+        for tb in late:
             o = opool.tile([P, N], F32, name="o", tag="o")
-            dst = out2d[rows, last_cb * N + c0 : last_cb * N + c0 + 128]
-            if i < 2:
-                rotate(
-                    o[:, 0:128].rearrange("p (h j) -> p h j", h=1),
-                    pieces[i][:, 0:128].rearrange("p (h j) -> p h j", h=1),
-                    last_tb,
-                    1,
-                )
-                nc.sync.dma_start(out=dst, in_=o[:, 0:128])
-            else:
-                nc.scalar.copy(out=o[:, 0:128], in_=pieces[i][:, 0:128])
-                nc.scalar.dma_start(out=dst, in_=o[:, 0:128])
+            o3 = o[:, 0:256].rearrange("p (h j) -> p h j", h=2)
+            rotate(o3, halves[(0, tb)][:, 0:256].rearrange("p (h j) -> p h j", h=2), tb, 2)
+            nc.sync.dma_start(out=out_block(tb, last_cb).rearrange("p (h c j) -> p h c j", h=2, c=2)[:, :, 1, :], in_=o3)
+        for tb in late:
+            o = opool.tile([P, N], F32, name="o", tag="o")
+            nc.scalar.copy(out=o[:, 0:256], in_=halves[(256, tb)][:, 0:256])
+            nc.scalar.dma_start(
+                out=out_block(tb, last_cb).rearrange("p (h c j) -> p h c j", h=2, c=2)[:, :, 0, :],
+                in_=o[:, 0:256].rearrange("p (h j) -> p h j", h=2),
+            )

@@ -20,7 +20,7 @@ PASSES = 8
 TOKEN_BLOCKS = 8
 COL_BLOCKS = 8
 N = 512
-WARM = 6
+WARM = 8
 RUNS = ((0, 2), (2, 5), (5, 8))
 
 
@@ -100,11 +100,10 @@ def tile_multiheadlatentattention_pb_kernel(tc, x_words, x_scales, Wq_words, Wq_
             )
 
         warm = keep.tile([P, N // 2], F32, name="warm")
+        nc.gpsimd.memset(warm[:], 0.0)
         for r in range(len(RUNS)):
             nc.vector.memset(xs[r][:].bitcast(I32), 0)
             nc.vector.memset(ws0[r][:].bitcast(I32), 0)
-            if r == 0:
-                nc.vector.memset(warm[:], 0.0)
         for cb in range(1, COL_BLOCKS - 1):
             nc.vector.memset(ws[cb][:].bitcast(I32), 0)
         nc.vector.memset(ws_stage[:].bitcast(I32), 0)

@@ -36,7 +36,7 @@ def tile_multiheadlatentattention_pb_kernel(tc, x_words, x_scales, Wq_words, Wq_
         psum = ctx.enter_context(tc.psum_pool(name="psum", bufs=8))
 
         def load_planes(dst, src, g0, g1, c0, c1):
-            for q in range(4):
+            for q in (0, 2, 1, 3):
                 nc.sync.dma_start(
                     out=dst[32 * q : 32 * q + 4, :, :].bitcast(I32),
                     in_=src[g0:g1, 4 * q : 4 * q + 4, c0:c1].rearrange("g r n -> r g n").bitcast(I32),

@@ -283,7 +283,10 @@ def tile_multiheadlatentattention_pb_kernel(tc, x_words, x_scales, Wq_words, Wq_
         for tb in late:
             o = opool.tile([P, N], F32, name="o", tag="o")
             nc.scalar.copy(out=o[:, 0:256], in_=halves[(256, tb)][:, 0:256])
-            nc.scalar.dma_start(
+            queue = nc.sync
+            if tb == TOKEN_BLOCKS - 1:
+                queue = nc.scalar
+            queue.dma_start(
                 out=out_block(tb, last_cb).rearrange("p (h c j) -> p h c j", h=2, c=2)[:, :, 0, :],
                 in_=o[:, 0:256].rearrange("p (h j) -> p h j", h=2),
             )

from contextlib import ExitStack

import concourse.mybir as mybir

FLOPS = 2 * 1024 * 4096 * 4096

F32 = mybir.dt.float32
BF16 = mybir.dt.bfloat16
I32 = mybir.dt.int32
U8 = mybir.dt.uint8
FP4X4 = mybir.dt.float4_e2m1fn_x4
ALU = mybir.AluOpType
ACT = mybir.ActivationFunctionType

PI = 3.141592653589793
ROPE_BASE = 10000.0

P = 128
PASSES = 8
TOKEN_BLOCKS = 8
COL_BLOCKS = 8
N = 512
WARM = 8
RUNS = ((0, 2), (2, 5), (5, 8))


def tile_multiheadlatentattention_pb_kernel(tc, x_words, x_scales, Wq_words, Wq_scales, out):
    nc = tc.nc
    out2d = out.rearrange("b s h d -> (b s) (h d)")

    with ExitStack() as ctx:
        ctx.enter_context(tc.manual_schedule())
        keep = ctx.enter_context(tc.tile_pool(name="keep", bufs=1))
        opool = ctx.enter_context(tc.tile_pool(name="opool", bufs=8))
        tpool = ctx.enter_context(tc.tile_pool(name="tpool", bufs=4))
        psum = ctx.enter_context(tc.psum_pool(name="psum", bufs=8))

        def load_planes(dst, src, g0, g1, c0, c1):
            for q in (0, 2, 1, 3):
                nc.sync.dma_start(
                    out=dst[32 * q : 32 * q + 4, :, :].bitcast(I32),
                    in_=src[g0:g1, 4 * q : 4 * q + 4, c0:c1].rearrange("g r n -> r g n").bitcast(I32),
                )

        xc = []
        wc0 = []
        for g in range(PASSES):
            xc.append(
                [
                    keep.tile([P, 1024], U8, name="xc%d_0" % g, align_bytes=64),
                    keep.tile([P, 1024], U8, name="xc%d_1" % g, align_bytes=64),
                ]
            )
            wc0.append(keep.tile([P, 2 * N], U8, name="wc0_%d" % g, align_bytes=64))
        xs = []
        ws0 = []
        for r in range(len(RUNS)):
            ng = RUNS[r][1] - RUNS[r][0]
            xs.append(keep.tile([P, ng, 1024], U8, name="xs%d" % r, align_bytes=64))
            ws0.append(keep.tile([P, ng, N], U8, name="ws0_%d" % r, align_bytes=64))
        wc = [None]
        ws = [None]
        for cb in range(1, COL_BLOCKS):
            wc.append(keep.tile([P, PASSES, 2 * N], U8, name="wc%d" % cb, align_bytes=64))
            ws.append(keep.tile([P, PASSES, N], U8, name="ws%d" % cb, align_bytes=64))

        wc_stage = keep.tile([P, PASSES, 2 * N], U8, name="wc_stage", align_bytes=64)
        ws_stage = keep.tile([P, PASSES, N], U8, name="ws_stage", align_bytes=64)

        def run_of(g):
            for r in range(len(RUNS)):
                if RUNS[r][0] <= g < RUNS[r][1]:
                    return r, g - RUNS[r][0]
            raise ValueError("pass out of range")

        def load_x_half(g, b):
            nc.sync.dma_start(out=xc[g][b][:].bitcast(I32), in_=x_words[g, :, b * 1024 : (b + 1) * 1024].bitcast(I32))

        def load_w0(g):
            nc.sync.dma_start(out=wc0[g][:].bitcast(I32), in_=Wq_words[g, :, 0 : 2 * N].bitcast(I32))

        def load_codes0(g):
            load_x_half(g, 0)
            load_w0(g)
            load_x_half(g, 1)

        def load_planes0(r):
            g0, g1 = RUNS[r]
            load_planes(xs[r], x_scales, g0, g1, 0, 1024)
            load_planes(ws0[r], Wq_scales, g0, g1, 0, N)

        def load_col_block(cb):
            codes, planes = wc[cb], ws[cb]
            if cb == COL_BLOCKS - 1:
                codes, planes = wc_stage, ws_stage
            load_planes(planes, Wq_scales, 0, PASSES, cb * N, (cb + 1) * N)
            nc.sync.dma_start(
                out=codes[:].bitcast(I32),
                in_=Wq_words[:, :, cb * 2 * N : (cb + 1) * 2 * N].rearrange("g p n -> p g n").bitcast(I32),
            )

        warm = keep.tile([P, N // 2], F32, name="warm")
        nc.gpsimd.memset(warm[:], 0.0)
        for r in range(len(RUNS)):
            nc.vector.memset(xs[r][:].bitcast(I32), 0)
            nc.vector.memset(ws0[r][:].bitcast(I32), 0)
        for cb in range(1, COL_BLOCKS - 1):
            nc.vector.memset(ws[cb][:].bitcast(I32), 0)
        nc.vector.memset(ws_stage[:].bitcast(I32), 0)

        load_x_half(0, 0)
        load_w0(0)
        load_planes0(0)
        load_x_half(0, 1)
        load_codes0(1)
        load_planes0(1)
        load_codes0(2)
        load_codes0(3)
        load_codes0(4)
        load_planes0(2)
        load_codes0(5)
        load_codes0(6)
        load_codes0(7)
        load_col_block(1)
        load_col_block(2)

        wacc = psum.tile([P, N], F32, name="acc", tag="acc")
        for i in range(WARM):
            nc.tensor.matmul(
                out=wacc[:], lhsT=warm[:].bitcast(BF16)[:, 0:P], rhs=warm[:].bitcast(BF16), start=True, stop=True
            )

        pos_i = keep.tile([P, 4], I32, name="pos_i")
        nc.gpsimd.iota(pos_i[:], pattern=[[128, 4]], base=0, channel_multiplier=1)
        pos_f = keep.tile([P, 4], F32, name="pos_f")
        nc.vector.tensor_copy(out=pos_f[:], in_=pos_i[:])
        turns = keep.tile([P, 4], F32, name="turns")
        nc.vector.tensor_scalar_mul(out=turns[:], in0=pos_f[:], scalar1=1.0 / (2.0 * PI))
        freq = keep.tile([P, 64], F32, name="freq")
        nc.vector.memset(freq[:, 0:1], 1.0)
        for k in range(6):
            n = 2**k
            nc.vector.tensor_scalar_mul(out=freq[:, n : 2 * n], in0=freq[:, 0:n], scalar1=ROPE_BASE ** (-n / 64.0))
        gdup = keep.tile([P, 2, 64, 2], F32, name="gdup")
        phase = keep.tile([P, 2, 64, 2], F32, name="phase")
        for w in range(2):
            for e in range(2):
                nc.vector.tensor_copy(out=gdup[:, w, :, e], in_=freq[:])
        nc.vector.memset(phase[:, 0, :, :], 0.0)
        nc.vector.memset(phase[:, 1, :, 0], -0.25)
        nc.vector.memset(phase[:, 1, :, 1], 0.25)
        u = keep.tile([P, 4, 256], F32, name="u")
        for a in range(4):
            nc.vector.scalar_tensor_tensor(
                out=u[:, a, :],
                in0=gdup[:].rearrange("p w i e -> p (w i e)"),
                scalar=turns[:, a : a + 1],
                in1=phase[:].rearrange("p w i e -> p (w i e)"),
                op0=ALU.mult,
                op1=ALU.add,
            )
        uflat = u[:].rearrange("p a j -> p (a j)")
        k_i = keep.tile([P, 1024], I32, name="k_i")
        nc.vector.tensor_copy(out=k_i[:], in_=uflat)
        k_f = keep.tile([P, 1024], F32, name="k_f")
        nc.vector.tensor_copy(out=k_f[:], in_=k_i[:])
        red = keep.tile([P, 1024], F32, name="red")
        nc.vector.tensor_sub(out=red[:], in0=uflat, in1=k_f[:])
        half_sin = keep.tile([P, 1024], F32, name="half_sin")
        nc.scalar.activation(out=half_sin[:], in_=red[:], func=ACT.Sin, scale=PI)
        m2sq = keep.tile([P, 1024], F32, name="m2sq")
        nc.vector.scalar_tensor_tensor(
            out=m2sq[:], in0=half_sin[:], scalar=-2.0, in1=half_sin[:], op0=ALU.mult, op1=ALU.mult
        )
        tab = keep.tile([P, 4, 2, 2, 128], F32, name="tab")
        for h in range(2):
            nc.vector.tensor_scalar_add(
                out=tab[:].rearrange("p a w h j -> p (a w) h j")[:, :, h, :],
                in0=m2sq[:].rearrange("p (m j) -> p m j", j=128),
                scalar1=1.0,
            )

        def one_pass(acc, g, tb, cb, c0, c1):
            r, gl = run_of(g)
            if cb == 0:
                rhs = wc0[g][:, 2 * c0 : 2 * c1]
                rhs_scale = ws0[r][:, gl, c0:c1]
            else:
                rhs = wc[cb][:, g, 2 * c0 : 2 * c1]
                rhs_scale = ws[cb][:, g, c0:c1]
            tl = tb % 4
            nc.tensor.matmul_mx(
                out=acc,
                lhsT=xc[g][tb // 4][:, tl * 256 : (tl + 1) * 256].bitcast(FP4X4),
                lhsT_scale=xs[r][:, gl, tb * 128 : (tb + 1) * 128],
                rhs=rhs.bitcast(FP4X4),
                rhs_scale=rhs_scale,
                start=(g == 0),
                stop=(g == PASSES - 1),
            )

        def rotate(dst, src, tb, heads):
            t = tpool.tile([P, 2, 256], F32, name="t", tag="t")
            for w in range(2):
                nc.vector.tensor_mul(
                    out=t[:, w, 0 : heads * 128].rearrange("p (h j) -> p h j", h=heads),
                    in0=src,
                    in1=tab[:, tb % 4, w, 0:heads, :],
                )
            nc.vector.tensor_add(
                out=dst.rearrange("p h (i e) -> p h i e", e=2),
                in0=t[:, 0, 0 : heads * 128].rearrange("p (h i e) -> p h i e", h=heads, e=2),
                in1=t[:, 1, 0 : heads * 128].rearrange("p (h i e) -> p h i e", h=heads, e=2)[:, :, :, ::-1],
            )

        last_cb = COL_BLOCKS - 1
        SPLIT = 2

        def regroup_last_block():
            for c in range(2):
                nc.vector.tensor_copy(
                    out=wc[last_cb][:].bitcast(I32).rearrange("p s (c h w) -> p s c h w", c=2, h=2)[:, :, 1 - c, :, :],
                    in_=wc_stage[:].bitcast(I32).rearrange("p s (h c w) -> p s h c w", h=2, c=2)[:, :, :, c, :],
                )
                nc.vector.tensor_copy(
                    out=ws[last_cb][:].bitcast(I32).rearrange("p s (c h w) -> p s c h w", c=2, h=2)[:, :, 1 - c, :, :],
                    in_=ws_stage[:].bitcast(I32).rearrange("p s (h c w) -> p s h c w", h=2, c=2)[:, :, :, c, :],
                )

        def out_block(tb, cb):
            return out2d[tb * P : (tb + 1) * P, cb * N : (cb + 1) * N]

        def epilogue(acc, tb, cb):
            o = opool.tile([P, N], F32, name="o", tag="o")
            o4 = o[:].rearrange("p (h c j) -> p h c j", h=2, c=2)
            if cb == last_cb:
                plain = acc[:, 256:512].rearrange("p (h j) -> p h j", h=2)
                turned = acc[:, 0:256].rearrange("p (h j) -> p h j", h=2)
            else:
                plain = acc[:].rearrange("p (h c j) -> p h c j", h=2, c=2)[:, :, 0, :]
                turned = acc[:].rearrange("p (h c j) -> p h c j", h=2, c=2)[:, :, 1, :]
            nc.scalar.copy(out=o4[:, :, 0, :], in_=plain)
            rotate(o4[:, :, 1, :], turned, tb, 2)
            nc.sync.dma_start(out=out_block(tb, cb), in_=o[:])

        first = []
        for tb in range(TOKEN_BLOCKS):
            first.append(psum.tile([P, N], F32, name="acc", tag="acc"))
        for g in range(PASSES):
            for tb in range(TOKEN_BLOCKS):
                one_pass(first[tb][:], g, tb, 0, 0, N)
        for tb in range(TOKEN_BLOCKS):
            epilogue(first[tb], tb, 0)
        load_col_block(3)

        for cb in range(1, COL_BLOCKS):
            whole = TOKEN_BLOCKS
            if cb == last_cb:
                whole = TOKEN_BLOCKS - SPLIT
            for tb in range(whole):
                acc = psum.tile([P, N], F32, name="acc", tag="acc")
                for g in range(PASSES):
                    one_pass(acc[:], g, tb, cb, 0, N)
                epilogue(acc, tb, cb)
            if cb + 3 < COL_BLOCKS:
                load_col_block(cb + 3)
            if cb + 2 == last_cb:
                regroup_last_block()

        late = range(TOKEN_BLOCKS - SPLIT, TOKEN_BLOCKS)
        halves = {}
        for c0 in (0, 256):
            for tb in late:
                acc = psum.tile([P, N], F32, name="acc", tag="acc")
                for g in range(PASSES):
                    one_pass(acc[:, 0:256], g, tb, last_cb, c0, c0 + 256)
                halves[(c0, tb)] = acc
        for tb in late:
            o = opool.tile([P, N], F32, name="o", tag="o")
            o3 = o[:, 0:256].rearrange("p (h j) -> p h j", h=2)
            rotate(o3, halves[(0, tb)][:, 0:256].rearrange("p (h j) -> p h j", h=2), tb, 2)
            nc.sync.dma_start(out=out_block(tb, last_cb).rearrange("p (h c j) -> p h c j", h=2, c=2)[:, :, 1, :], in_=o3)
        for tb in late:
            o = opool.tile([P, N], F32, name="o", tag="o")
            nc.scalar.copy(out=o[:, 0:256], in_=halves[(256, tb)][:, 0:256])
            queue = nc.sync
            if tb == TOKEN_BLOCKS - 1:
                queue = nc.scalar
            queue.dma_start(
                out=out_block(tb, last_cb).rearrange("p (h c j) -> p h c j", h=2, c=2)[:, :, 0, :],
                in_=o[:, 0:256].rearrange("p (h j) -> p h j", h=2),
            )
